import numpy as np
import ml_dtypes

BF16 = ml_dtypes.bfloat16


def bf(x):
    return np.asarray(x, np.float32).astype(BF16)


def f32(x):
    return np.asarray(x, np.float32)


def f64(x):
    return np.asarray(x).astype(np.float64)


def striped(idx):
    return np.tile(idx.reshape(-1, 16).T, (8, 1))


C, S, N, M = 512, 256, 256, 256
TAGS = 5.0


def setup_inputs():
    return {"cand_emb": f32(np.random.standard_normal((C, S))), "auth_emb": f32(np.random.standard_normal((C, N))), "tag_sum": f32(2.0 * np.random.standard_normal((C, N))), "w": bf(np.random.standard_normal((C, M)) / np.sqrt(C)), "b": f32(0.1 * np.random.standard_normal((M, 1))), "offs": striped(np.random.permutation(np.tile(np.arange(S), 2))[:N])}


def reference(cand_emb, auth_emb, tag_sum, w, b, offs):
    idx = offs[:16].T.reshape(-1)
    v = f64(cand_emb)[:, idx] + f64(auth_emb) + f64(tag_sum) / TAGS
    return np.maximum(f64(w).T @ v + f64(b), 0.0)

@@ -1,0 +1,61 @@
+import concourse.mybir as mybir
+
+F32, BF16, U16 = mybir.dt.float32, mybir.dt.bfloat16, mybir.dt.uint16
+ADD, MULT = mybir.AluOpType.add, mybir.AluOpType.mult
+RELU = mybir.ActivationFunctionType.Relu
+
+P = 128
+C, S, N, M = 512, 256, 256, 256
+C_BLOCKS = C // P
+M_BLOCKS = M // P
+TAGS = 5.0
+
+FLOPS = 2 * C * M * N
+
+
+def tile_dlrm_kernel(tc, cand_emb, auth_emb, tag_sum, w, b, offs, out):
+    nc = tc.nc
+    with (
+        tc.tile_pool(name="held", bufs=1) as held,
+        tc.tile_pool(name="blocks", bufs=C_BLOCKS) as blocks,
+        tc.psum_pool(name="psum", bufs=1) as psum,
+    ):
+        offsets = held.tile([P, N // 16], U16, name="offsets")
+        nc.sync.dma_start(offsets[:], offs)
+
+        bias = held.tile([P, M_BLOCKS], F32, name="bias")
+        with nc.allow_non_contiguous_dma(reason="256 single floats, one to a partition"):
+            nc.gpsimd.dma_start(bias[:], b.rearrange("(h p) one -> p (h one)", p=P))
+
+        acc = [psum.tile([P, N], F32, name=f"acc{h}") for h in range(M_BLOCKS)]
+
+        for k in range(C_BLOCKS):
+            rows = slice(k * P, (k + 1) * P)
+            table = blocks.tile([P, S], F32, name="table")
+            author = blocks.tile([P, N], F32, name="author")
+            tags = blocks.tile([P, N], F32, name="tags")
+            weights = blocks.tile([P, M], BF16, name="weights")
+            nc.sync.dma_start(table[:], cand_emb[rows, :])
+            nc.scalar.dma_start(author[:], auth_emb[rows, :])
+            nc.sync.dma_start(tags[:], tag_sum[rows, :])
+            nc.scalar.dma_start(weights[:], w[rows, :])
+
+            book_author = blocks.tile([P, N], F32, name="book_author")
+            nc.vector.tensor_tensor(book_author[:], table[:].indirect(offsets[:]), author[:], ADD)
+
+            v = blocks.tile([P, N], BF16, name="v")
+            nc.vector.scalar_tensor_tensor(v[:], tags[:], 1.0 / TAGS, book_author[:], MULT, ADD)
+
+            for h in range(M_BLOCKS):
+                nc.tensor.matmul(
+                    acc[h][:],
+                    weights[:, h * P : (h + 1) * P],
+                    v[:],
+                    start=(k == 0),
+                    stop=(k == C_BLOCKS - 1),
+                )
+
+        for h in range(M_BLOCKS):
+            result = blocks.tile([P, N], F32, name="result")
+            nc.scalar.activation(result[:], acc[h][:], RELU, bias=bias[:, h : h + 1])
+            nc.sync.dma_start(out[h * P : (h + 1) * P, :], result[:])

@@ -1,7 +1,7 @@
 import concourse.mybir as mybir
 
 F32, BF16, U16 = mybir.dt.float32, mybir.dt.bfloat16, mybir.dt.uint16
-ADD, MULT = mybir.AluOpType.add, mybir.AluOpType.mult
+ADD, MULT, MAX = mybir.AluOpType.add, mybir.AluOpType.mult, mybir.AluOpType.max
 RELU = mybir.ActivationFunctionType.Relu
 
 P = 128
@@ -17,7 +17,6 @@ def tile_dlrm_kernel(tc, cand_emb, auth_emb, tag_sum, w, b, offs, out):
     nc = tc.nc
     with (
         tc.tile_pool(name="held", bufs=1) as held,
-        tc.tile_pool(name="blocks", bufs=C_BLOCKS) as blocks,
         tc.psum_pool(name="psum", bufs=1) as psum,
     ):
         offsets = held.tile([P, N // 16], U16, name="offsets")
@@ -25,37 +24,53 @@ def tile_dlrm_kernel(tc, cand_emb, auth_emb, tag_sum, w, b, offs, out):
 
         bias = held.tile([P, M_BLOCKS], F32, name="bias")
         with nc.allow_non_contiguous_dma(reason="256 single floats, one to a partition"):
-            nc.gpsimd.dma_start(bias[:], b.rearrange("(h p) one -> p (h one)", p=P))
+            nc.scalar.dma_start(bias[:], b.rearrange("(h p) one -> p (h one)", p=P))
 
+        table = [held.tile([P, S], F32, name=f"table{k}") for k in range(C_BLOCKS)]
+        author = [held.tile([P, N], F32, name=f"author{k}") for k in range(C_BLOCKS)]
+        tags = [held.tile([P, N], F32, name=f"tags{k}") for k in range(C_BLOCKS)]
+        weights = [held.tile([P, M], BF16, name=f"weights{k}") for k in range(C_BLOCKS)]
         acc = [psum.tile([P, N], F32, name=f"acc{h}") for h in range(M_BLOCKS)]
+        book_author = [held.tile([P, N], F32, name=f"book_author{k}") for k in range(C_BLOCKS)]
+        v = [held.tile([P, N], BF16, name=f"v{k}") for k in range(C_BLOCKS)]
+        result = [held.tile([P, N], F32, name=f"result{h}") for h in range(M_BLOCKS)]
 
-        for k in range(C_BLOCKS):
+        def load_for_look_up(k):
             rows = slice(k * P, (k + 1) * P)
-            table = blocks.tile([P, S], F32, name="table")
-            author = blocks.tile([P, N], F32, name="author")
-            tags = blocks.tile([P, N], F32, name="tags")
-            weights = blocks.tile([P, M], BF16, name="weights")
-            nc.sync.dma_start(table[:], cand_emb[rows, :])
-            nc.scalar.dma_start(author[:], auth_emb[rows, :])
-            nc.sync.dma_start(tags[:], tag_sum[rows, :])
-            nc.scalar.dma_start(weights[:], w[rows, :])
+            nc.sync.dma_start(table[k][:], cand_emb[rows, :])
+            nc.sync.dma_start(author[k][:], auth_emb[rows, :])
 
-            book_author = blocks.tile([P, N], F32, name="book_author")
-            nc.vector.tensor_tensor(book_author[:], table[:].indirect(offsets[:]), author[:], ADD)
+        def load_for_finish(k):
+            rows = slice(k * P, (k + 1) * P)
+            nc.sync.dma_start(tags[k][:], tag_sum[rows, :])
+            nc.sync.dma_start(weights[k][:], w[rows, :])
 
-            v = blocks.tile([P, N], BF16, name="v")
-            nc.vector.scalar_tensor_tensor(v[:], tags[:], 1.0 / TAGS, book_author[:], MULT, ADD)
+        def look_up(k):
+            nc.vector.tensor_tensor(book_author[k][:], table[k][:].indirect(offsets[:]), author[k][:], ADD)
 
+        def finish(k):
+            nc.vector.scalar_tensor_tensor(v[k][:], tags[k][:], 1.0 / TAGS, book_author[k][:], MULT, ADD)
             for h in range(M_BLOCKS):
                 nc.tensor.matmul(
                     acc[h][:],
-                    weights[:, h * P : (h + 1) * P],
-                    v[:],
+                    weights[k][:, h * P : (h + 1) * P],
+                    v[k][:],
                     start=(k == 0),
                     stop=(k == C_BLOCKS - 1),
                 )
 
+        load_for_look_up(0)
+        for k in range(1, C_BLOCKS):
+            load_for_look_up(k)
+            load_for_finish(k - 1)
+        load_for_finish(C_BLOCKS - 1)
+
+        look_up(0)
+        for k in range(1, C_BLOCKS):
+            look_up(k)
+            finish(k - 1)
+        finish(C_BLOCKS - 1)
+
         for h in range(M_BLOCKS):
-            result = blocks.tile([P, N], F32, name="result")
-            nc.scalar.activation(result[:], acc[h][:], RELU, bias=bias[:, h : h + 1])
-            nc.sync.dma_start(out[h * P : (h + 1) * P, :], result[:])
+            nc.scalar.activation(result[h][:], acc[h][:], RELU, bias=bias[:, h : h + 1])
+            nc.sync.dma_start(out[h * P : (h + 1) * P, :], result[h][:])

@@ -38,12 +38,12 @@ def tile_dlrm_kernel(tc, cand_emb, auth_emb, tag_sum, w, b, offs, out):
         def load_for_look_up(k):
             rows = slice(k * P, (k + 1) * P)
             nc.sync.dma_start(table[k][:], cand_emb[rows, :])
-            nc.sync.dma_start(author[k][:], auth_emb[rows, :])
+            nc.scalar.dma_start(author[k][:], auth_emb[rows, :])
 
         def load_for_finish(k):
             rows = slice(k * P, (k + 1) * P)
             nc.sync.dma_start(tags[k][:], tag_sum[rows, :])
-            nc.sync.dma_start(weights[k][:], w[rows, :])
+            nc.scalar.dma_start(weights[k][:], w[rows, :])
 
         def look_up(k):
             nc.vector.tensor_tensor(book_author[k][:], table[k][:].indirect(offsets[:]), author[k][:], ADD)

@@ -8,6 +8,8 @@ P = 128
 C, S, N, M = 512, 256, 256, 256
 C_BLOCKS = C // P
 M_BLOCKS = M // P
+N_PIECES = 2
+PIECE = N // N_PIECES
 TAGS = 5.0
 
 FLOPS = 2 * C * M * N
@@ -30,10 +32,13 @@ def tile_dlrm_kernel(tc, cand_emb, auth_emb, tag_sum, w, b, offs, out):
         author = [held.tile([P, N], F32, name=f"author{k}") for k in range(C_BLOCKS)]
         tags = [held.tile([P, N], F32, name=f"tags{k}") for k in range(C_BLOCKS)]
         weights = [held.tile([P, M], BF16, name=f"weights{k}") for k in range(C_BLOCKS)]
-        acc = [psum.tile([P, N], F32, name=f"acc{h}") for h in range(M_BLOCKS)]
         book_author = [held.tile([P, N], F32, name=f"book_author{k}") for k in range(C_BLOCKS)]
         v = [held.tile([P, N], BF16, name=f"v{k}") for k in range(C_BLOCKS)]
         result = [held.tile([P, N], F32, name=f"result{h}") for h in range(M_BLOCKS)]
+        acc = [
+            [psum.tile([P, PIECE], F32, name=f"acc{h}_{c}") for c in range(N_PIECES)]
+            for h in range(M_BLOCKS)
+        ]
 
         def load_for_look_up(k):
             rows = slice(k * P, (k + 1) * P)
@@ -49,15 +54,19 @@ def tile_dlrm_kernel(tc, cand_emb, auth_emb, tag_sum, w, b, offs, out):
             nc.vector.tensor_tensor(book_author[k][:], table[k][:].indirect(offsets[:]), author[k][:], ADD)
 
         def finish(k):
-            nc.vector.scalar_tensor_tensor(v[k][:], tags[k][:], 1.0 / TAGS, book_author[k][:], MULT, ADD)
-            for h in range(M_BLOCKS):
-                nc.tensor.matmul(
-                    acc[h][:],
-                    weights[k][:, h * P : (h + 1) * P],
-                    v[k][:],
-                    start=(k == 0),
-                    stop=(k == C_BLOCKS - 1),
+            for c in range(N_PIECES):
+                cols = slice(c * PIECE, (c + 1) * PIECE)
+                nc.vector.scalar_tensor_tensor(
+                    v[k][:, cols], tags[k][:, cols], 1.0 / TAGS, book_author[k][:, cols], MULT, ADD
                 )
+                for h in range(M_BLOCKS):
+                    nc.tensor.matmul(
+                        acc[h][c][:],
+                        weights[k][:, h * P : (h + 1) * P],
+                        v[k][:, cols],
+                        start=(k == 0),
+                        stop=(k == C_BLOCKS - 1),
+                    )
 
         load_for_look_up(0)
         for k in range(1, C_BLOCKS):
@@ -71,6 +80,9 @@ def tile_dlrm_kernel(tc, cand_emb, auth_emb, tag_sum, w, b, offs, out):
             finish(k - 1)
         finish(C_BLOCKS - 1)
 
-        for h in range(M_BLOCKS):
-            nc.scalar.activation(result[h][:], acc[h][:], RELU, bias=bias[:, h : h + 1])
-            nc.sync.dma_start(out[h * P : (h + 1) * P, :], result[h][:])
+        for c in range(N_PIECES):
+            cols = slice(c * PIECE, (c + 1) * PIECE)
+            nc.scalar.activation(result[0][:, cols], acc[0][c][:], RELU, bias=bias[:, 0:1])
+            nc.scalar.dma_start(out[0:P, cols], result[0][:, cols])
+            nc.vector.tensor_scalar(result[1][:, cols], acc[1][c][:], bias[:, 1:2], 0.0, ADD, MAX)
+            nc.sync.dma_start(out[P : 2 * P, cols], result[1][:, cols])

@@ -8,8 +8,6 @@ P = 128
 C, S, N, M = 512, 256, 256, 256
 C_BLOCKS = C // P
 M_BLOCKS = M // P
-N_PIECES = 2
-PIECE = N // N_PIECES
 TAGS = 5.0
 
 FLOPS = 2 * C * M * N
@@ -24,21 +22,19 @@ def tile_dlrm_kernel(tc, cand_emb, auth_emb, tag_sum, w, b, offs, out):
         offsets = held.tile([P, N // 16], U16, name="offsets")
         nc.sync.dma_start(offsets[:], offs)
 
-        bias = held.tile([P, M_BLOCKS], F32, name="bias")
-        with nc.allow_non_contiguous_dma(reason="256 single floats, one to a partition"):
-            nc.scalar.dma_start(bias[:], b.rearrange("(h p) one -> p (h one)", p=P))
+        bias_row = held.tile([1, M], F32, name="bias_row")
+        nc.scalar.dma_start(bias_row[:], b.rearrange("m one -> one m"))
+        ones_row = held.tile([1, N], F32, name="ones_row")
+        nc.gpsimd.memset(ones_row[:], 1.0)
 
         table = [held.tile([P, S], F32, name=f"table{k}") for k in range(C_BLOCKS)]
         author = [held.tile([P, N], F32, name=f"author{k}") for k in range(C_BLOCKS)]
         tags = [held.tile([P, N], F32, name=f"tags{k}") for k in range(C_BLOCKS)]
         weights = [held.tile([P, M], BF16, name=f"weights{k}") for k in range(C_BLOCKS)]
+        acc = [psum.tile([P, N], F32, name=f"acc{h}") for h in range(M_BLOCKS)]
         book_author = [held.tile([P, N], F32, name=f"book_author{k}") for k in range(C_BLOCKS)]
         v = [held.tile([P, N], BF16, name=f"v{k}") for k in range(C_BLOCKS)]
         result = [held.tile([P, N], F32, name=f"result{h}") for h in range(M_BLOCKS)]
-        acc = [
-            [psum.tile([P, PIECE], F32, name=f"acc{h}_{c}") for c in range(N_PIECES)]
-            for h in range(M_BLOCKS)
-        ]
 
         def load_for_look_up(k):
             rows = slice(k * P, (k + 1) * P)
@@ -54,19 +50,15 @@ def tile_dlrm_kernel(tc, cand_emb, auth_emb, tag_sum, w, b, offs, out):
             nc.vector.tensor_tensor(book_author[k][:], table[k][:].indirect(offsets[:]), author[k][:], ADD)
 
         def finish(k):
-            for c in range(N_PIECES):
-                cols = slice(c * PIECE, (c + 1) * PIECE)
-                nc.vector.scalar_tensor_tensor(
-                    v[k][:, cols], tags[k][:, cols], 1.0 / TAGS, book_author[k][:, cols], MULT, ADD
+            nc.vector.scalar_tensor_tensor(v[k][:], tags[k][:], 1.0 / TAGS, book_author[k][:], MULT, ADD)
+            for h in range(M_BLOCKS):
+                nc.tensor.matmul(
+                    acc[h][:],
+                    weights[k][:, h * P : (h + 1) * P],
+                    v[k][:],
+                    start=False,
+                    stop=(k == C_BLOCKS - 1),
                 )
-                for h in range(M_BLOCKS):
-                    nc.tensor.matmul(
-                        acc[h][c][:],
-                        weights[k][:, h * P : (h + 1) * P],
-                        v[k][:, cols],
-                        start=(k == 0),
-                        stop=(k == C_BLOCKS - 1),
-                    )
 
         load_for_look_up(0)
         for k in range(1, C_BLOCKS):
@@ -74,15 +66,15 @@ def tile_dlrm_kernel(tc, cand_emb, auth_emb, tag_sum, w, b, offs, out):
             load_for_finish(k - 1)
         load_for_finish(C_BLOCKS - 1)
 
+        for h in range(M_BLOCKS):
+            nc.tensor.matmul(acc[h][:], bias_row[:, h * P : (h + 1) * P], ones_row[:], start=True, stop=False)
+
         look_up(0)
         for k in range(1, C_BLOCKS):
             look_up(k)
             finish(k - 1)
         finish(C_BLOCKS - 1)
 
-        for c in range(N_PIECES):
-            cols = slice(c * PIECE, (c + 1) * PIECE)
-            nc.scalar.activation(result[0][:, cols], acc[0][c][:], RELU, bias=bias[:, 0:1])
-            nc.scalar.dma_start(out[0:P, cols], result[0][:, cols])
-            nc.vector.tensor_scalar(result[1][:, cols], acc[1][c][:], bias[:, 1:2], 0.0, ADD, MAX)
-            nc.sync.dma_start(out[P : 2 * P, cols], result[1][:, cols])
+        for h in range(M_BLOCKS):
+            nc.scalar.activation(result[h][:], acc[h][:], RELU)
+            nc.sync.dma_start(out[h * P : (h + 1) * P, :], result[h][:])

@@ -24,8 +24,8 @@ def tile_dlrm_kernel(tc, cand_emb, auth_emb, tag_sum, w, b, offs, out):
 
         bias_row = held.tile([1, M], F32, name="bias_row")
         nc.scalar.dma_start(bias_row[:], b.rearrange("m one -> one m"))
-        ones_row = held.tile([1, N], F32, name="ones_row")
-        nc.gpsimd.memset(ones_row[:], 1.0)
+        one = held.tile([1, 1], F32, name="one")
+        nc.gpsimd.memset(one[:], 1.0)
 
         table = [held.tile([P, S], F32, name=f"table{k}") for k in range(C_BLOCKS)]
         author = [held.tile([P, N], F32, name=f"author{k}") for k in range(C_BLOCKS)]
@@ -56,7 +56,7 @@ def tile_dlrm_kernel(tc, cand_emb, auth_emb, tag_sum, w, b, offs, out):
                     acc[h][:],
                     weights[k][:, h * P : (h + 1) * P],
                     v[k][:],
-                    start=False,
+                    start=(k == 0),
                     stop=(k == C_BLOCKS - 1),
                 )
 
@@ -66,15 +66,18 @@ def tile_dlrm_kernel(tc, cand_emb, auth_emb, tag_sum, w, b, offs, out):
             load_for_finish(k - 1)
         load_for_finish(C_BLOCKS - 1)
 
-        for h in range(M_BLOCKS):
-            nc.tensor.matmul(acc[h][:], bias_row[:, h * P : (h + 1) * P], ones_row[:], start=True, stop=False)
-
         look_up(0)
         for k in range(1, C_BLOCKS):
             look_up(k)
             finish(k - 1)
         finish(C_BLOCKS - 1)
 
+        bias_psum = psum.tile([P, M_BLOCKS], F32, name="bias_psum")
         for h in range(M_BLOCKS):
-            nc.scalar.activation(result[h][:], acc[h][:], RELU)
+            nc.tensor.matmul(bias_psum[:, h : h + 1], bias_row[:, h * P : (h + 1) * P], one[:], start=True, stop=True)
+        bias = held.tile([P, M_BLOCKS], F32, name="bias")
+        nc.vector.tensor_copy(bias[:], bias_psum[:])
+
+        for h in range(M_BLOCKS):
+            nc.scalar.activation(result[h][:], acc[h][:], RELU, bias=bias[:, h : h + 1])
             nc.sync.dma_start(out[h * P : (h + 1) * P, :], result[h][:])

@@ -66,17 +66,17 @@ def tile_dlrm_kernel(tc, cand_emb, auth_emb, tag_sum, w, b, offs, out):
             load_for_finish(k - 1)
         load_for_finish(C_BLOCKS - 1)
 
-        look_up(0)
-        for k in range(1, C_BLOCKS):
-            look_up(k)
-            finish(k - 1)
-        finish(C_BLOCKS - 1)
-
         bias_psum = psum.tile([P, M_BLOCKS], F32, name="bias_psum")
         for h in range(M_BLOCKS):
             nc.tensor.matmul(bias_psum[:, h : h + 1], bias_row[:, h * P : (h + 1) * P], one[:], start=True, stop=True)
         bias = held.tile([P, M_BLOCKS], F32, name="bias")
         nc.vector.tensor_copy(bias[:], bias_psum[:])
+
+        look_up(0)
+        for k in range(1, C_BLOCKS):
+            look_up(k)
+            finish(k - 1)
+        finish(C_BLOCKS - 1)
 
         for h in range(M_BLOCKS):
             nc.scalar.activation(result[h][:], acc[h][:], RELU, bias=bias[:, h : h + 1])

import concourse.mybir as mybir

F32, BF16, U16 = mybir.dt.float32, mybir.dt.bfloat16, mybir.dt.uint16
ADD, MULT, MAX = mybir.AluOpType.add, mybir.AluOpType.mult, mybir.AluOpType.max
RELU = mybir.ActivationFunctionType.Relu

P = 128
C, S, N, M = 512, 256, 256, 256
C_BLOCKS = C // P
M_BLOCKS = M // P
TAGS = 5.0

FLOPS = 2 * C * M * N


def tile_dlrm_kernel(tc, cand_emb, auth_emb, tag_sum, w, b, offs, out):
    nc = tc.nc
    with (
        tc.tile_pool(name="held", bufs=1) as held,
        tc.psum_pool(name="psum", bufs=1) as psum,
    ):
        offsets = held.tile([P, N // 16], U16, name="offsets")
        nc.sync.dma_start(offsets[:], offs)

        bias_row = held.tile([1, M], F32, name="bias_row")
        nc.scalar.dma_start(bias_row[:], b.rearrange("m one -> one m"))
        one = held.tile([1, 1], F32, name="one")
        nc.gpsimd.memset(one[:], 1.0)

        table = [held.tile([P, S], F32, name=f"table{k}") for k in range(C_BLOCKS)]
        author = [held.tile([P, N], F32, name=f"author{k}") for k in range(C_BLOCKS)]
        tags = [held.tile([P, N], F32, name=f"tags{k}") for k in range(C_BLOCKS)]
        weights = [held.tile([P, M], BF16, name=f"weights{k}") for k in range(C_BLOCKS)]
        acc = [psum.tile([P, N], F32, name=f"acc{h}") for h in range(M_BLOCKS)]
        book_author = [held.tile([P, N], F32, name=f"book_author{k}") for k in range(C_BLOCKS)]
        v = [held.tile([P, N], BF16, name=f"v{k}") for k in range(C_BLOCKS)]
        result = [held.tile([P, N], F32, name=f"result{h}") for h in range(M_BLOCKS)]

        def load_for_look_up(k):
            rows = slice(k * P, (k + 1) * P)
            nc.sync.dma_start(table[k][:], cand_emb[rows, :])
            nc.scalar.dma_start(author[k][:], auth_emb[rows, :])

        def load_for_finish(k):
            rows = slice(k * P, (k + 1) * P)
            nc.sync.dma_start(tags[k][:], tag_sum[rows, :])
            nc.scalar.dma_start(weights[k][:], w[rows, :])

        def look_up(k):
            nc.vector.tensor_tensor(book_author[k][:], table[k][:].indirect(offsets[:]), author[k][:], ADD)

        def finish(k):
            nc.vector.scalar_tensor_tensor(v[k][:], tags[k][:], 1.0 / TAGS, book_author[k][:], MULT, ADD)
            for h in range(M_BLOCKS):
                nc.tensor.matmul(
                    acc[h][:],
                    weights[k][:, h * P : (h + 1) * P],
                    v[k][:],
                    start=(k == 0),
                    stop=(k == C_BLOCKS - 1),
                )

        load_for_look_up(0)
        for k in range(1, C_BLOCKS):
            load_for_look_up(k)
            load_for_finish(k - 1)
        load_for_finish(C_BLOCKS - 1)

        bias_psum = psum.tile([P, M_BLOCKS], F32, name="bias_psum")
        for h in range(M_BLOCKS):
            nc.tensor.matmul(bias_psum[:, h : h + 1], bias_row[:, h * P : (h + 1) * P], one[:], start=True, stop=True)
        bias = held.tile([P, M_BLOCKS], F32, name="bias")
        nc.vector.tensor_copy(bias[:], bias_psum[:])

        look_up(0)
        for k in range(1, C_BLOCKS):
            look_up(k)
            finish(k - 1)
        finish(C_BLOCKS - 1)

        for h in range(M_BLOCKS):
            nc.scalar.activation(result[h][:], acc[h][:], RELU, bias=bias[:, h : h + 1])
            nc.sync.dma_start(out[h * P : (h + 1) * P, :], result[h][:])
